import numpy as np
import ml_dtypes


def mxq(x, axis, fmt="e4m3"):
    dtype, down = {"e4m3": (ml_dtypes.float8_e4m3fn, 7), "e5m2": (ml_dtypes.float8_e5m2, 14)}[fmt]
    v = np.moveaxis(np.asarray(x, np.float32).astype(ml_dtypes.bfloat16).astype(np.float64), axis, -1)
    blocks = v.reshape(v.shape[:-1] + (-1, 32))
    amax = np.abs(blocks).max(-1, keepdims=True)
    byte = np.maximum(np.where(amax > 0, np.frexp(amax)[1] - 1 + 127, 0) - down, 1)
    scale = np.exp2(byte - 127.0)
    codes = (blocks / scale).astype(np.float32).astype(dtype).astype(np.float64)
    return np.moveaxis((codes * scale).reshape(v.shape), -1, axis)


WIDE = False


def mx_kscale(k):
    if not WIDE:
        return np.ones(k)
    levels = np.array([10, -10, 5, -5, 0])
    if k % 512:
        return np.exp2(np.random.permutation(np.resize(levels, k // 32))).repeat(32)
    a = np.empty((k // 512, 16))
    for p in range(k // 512):
        a[p, :8] = np.random.permutation(np.resize(levels, 8))
        for g in range(8):
            far = levels[np.abs(levels - a[p, g]) >= 10]
            a[p, g + 8] = far[np.random.randint(len(far))]
    return np.exp2(a.ravel()).repeat(32)


BF16 = ml_dtypes.bfloat16


def bf(x):
    return np.asarray(x, np.float32).astype(BF16)


def f64(x):
    return np.asarray(x).astype(np.float64)


E2M1 = np.array([0.0, 0.5, 1.0, 1.5, 2.0, 3.0, 4.0, 6.0, -0.0, -0.5, -1.0, -1.5, -2.0, -3.0, -4.0, -6.0])


def pack_weight(w, fmt):
    k, n = w.shape
    w = f64(bf(w)).reshape(k // 32, 32, n)
    amax = np.abs(w).max(1)
    if fmt == "e4m3":
        byte = np.frexp(amax)[1] - 1 + 127 - 7
    else:
        mant, ex = np.frexp(amax / 6.0)
        byte = np.where(mant > 0.5, ex, ex - 1) + 127
    byte = np.clip(np.where(amax > 0, byte, 1), 1, 254)
    scaled = (w * np.exp2(127.0 - byte)[:, None, :]).reshape(k, n).astype(np.float32)
    by_word = np.ascontiguousarray(scaled.reshape(k // 512, 128, 4, n).transpose(0, 1, 3, 2))
    if fmt == "e4m3":
        words = by_word.astype(ml_dtypes.float8_e4m3fn).view(np.uint8)
    else:
        c = by_word.astype(ml_dtypes.float4_e2m1fn).view(np.uint8) & 0xF
        words = c[..., 0::2] | (c[..., 1::2] << 4)
    return np.ascontiguousarray(words), np.ascontiguousarray(byte.astype(np.uint8).reshape(k // 512, 16, n))


def unpack_weight(words, scales, fmt):
    g, p, n, _ = words.shape
    if fmt == "e4m3":
        vals = np.ascontiguousarray(words).view(ml_dtypes.float8_e4m3fn).astype(np.float64)
    else:
        nib = np.empty((g, p, n, 4), np.uint8)
        nib[..., 0::2] = words & 0xF
        nib[..., 1::2] = words >> 4
        vals = E2M1[nib]
    vals = vals * np.repeat(np.exp2(scales.astype(np.float64) - 127.0), 8, axis=1)[..., None]
    return vals.transpose(0, 1, 3, 2).reshape(g * 512, n)
def pack4(w):
    words, scales = pack_weight(w, "e2m1")
    return words.reshape(words.shape[0], 128, -1), scales


def unpack4(words, scales):
    return unpack_weight(words.reshape(words.shape[0], 128, -1, 2), scales, "e2m1")


B, G, C, F, NC = 128, 6, 1024, 1024, 4096
HW = G * G
P_GEM = 3.0
EPS_GEM = 1e-6
EPS_NORM = 1e-12


def l2n(v, axis):
    n = np.sqrt(np.sum(v * v, axis=axis, keepdims=True))
    return v / np.maximum(n, EPS_NORM)


def draw0():
    s, t = mx_kscale(F), mx_kscale(C)
    z = np.random.standard_normal((B, HW, F))
    fc2_w_words, fc2_w_scales = pack4(np.random.standard_normal((F, C)) * 1.5 / np.sqrt(F) / s[:, None] * t)
    fc2_b = bf(np.random.standard_normal(C) * 0.3 * t)
    head_w_words, head_w_scales = pack4(np.random.standard_normal((C, NC)) / np.sqrt(C) / t[:, None])
    return {"hdn": bf(z / (1.0 + np.exp(-1.702 * z)) * s),
            "fc2_w_words": fc2_w_words,
            "fc2_w_scales": fc2_w_scales,
            "fc2_b": fc2_b,
            "head_w_words": head_w_words,
            "head_w_scales": head_w_scales,
            "head_b": bf(np.random.standard_normal(NC) * 0.3)}


def core(hdn, fc2_w_words, fc2_w_scales, fc2_b, head_w_words, head_w_scales, head_b):
    tok = (mxq(f64(hdn), 2, "e4m3") @ unpack4(fc2_w_words, fc2_w_scales)) + f64(fc2_b)
    g = np.mean(np.maximum(tok, EPS_GEM) ** P_GEM, axis=1) ** (1.0 / P_GEM)
    desc = (mxq(g, 1, "e4m3") @ unpack4(head_w_words, head_w_scales)) + f64(head_b)
    return l2n(desc, 1)


def e4m3fn_bytes(y):
    return np.clip(np.asarray(y, np.float64), -448.0, 448.0).astype(np.float32).astype(ml_dtypes.float8_e4m3fn).view(np.uint8)


def e4m3fn_values(b):
    return np.asarray(b, np.uint8).view(ml_dtypes.float8_e4m3fn).astype(np.float64)


def setup_inputs():
    d = draw0()
    x0 = np.asarray(d['hdn']).astype(np.float64)
    s = (np.max(np.abs(x0), axis=(0, 1), keepdims=True) / 448.0).astype(np.float32)
    out = {}
    for k, v in d.items():
        if k == 'hdn':
            out['hdn_bytes'] = e4m3fn_bytes(x0 / s.astype(np.float64))
            out['hdn_scale'] = s
        else:
            out[k] = v
    return out


def reference(hdn_bytes, hdn_scale, fc2_w_words, fc2_w_scales, fc2_b, head_w_words, head_w_scales, head_b):
    return core(e4m3fn_values(hdn_bytes) * hdn_scale.astype(np.float64), fc2_w_words, fc2_w_scales, fc2_b, head_w_words, head_w_scales, head_b)

@@ -1,0 +1,323 @@
+from contextlib import ExitStack
+
+import concourse.mybir as mybir
+from concourse.masks import make_identity
+
+IMAGES, TOKENS, HIDDEN, CHANNELS, OUT = 128, 36, 1024, 1024, 4096
+FLOPS = 2 * IMAGES * TOKENS * HIDDEN * CHANNELS + 2 * IMAGES * CHANNELS * OUT
+
+F32 = mybir.dt.float32
+BF16 = mybir.dt.bfloat16
+I32 = mybir.dt.int32
+U32 = mybir.dt.uint32
+U8 = mybir.dt.uint8
+FP8 = mybir.dt.float8_e4m3fn
+FP8X4 = mybir.dt.float8_e4m3fn_x4
+FP4X4 = mybir.dt.float4_e2m1fn_x4
+ALU = mybir.AluOpType
+ACT = mybir.ActivationFunctionType
+AX = mybir.AxisListType
+
+P = 128
+EPS = 1e-6
+EPS_CUBE = 1e-18
+STEPS = 9
+UNITS = 18
+
+
+def tile_tokenmudule_pb_w4_kernel(
+    tc, hdn_bytes, hdn_scale, fc2_w_words, fc2_w_scales, fc2_b, head_w_words, head_w_scales, head_b, out
+):
+    nc = tc.nc
+    with ExitStack() as ctx:
+        keep = ctx.enter_context(tc.tile_pool(name="keep", bufs=1))
+        work = ctx.enter_context(tc.tile_pool(name="work", bufs=2))
+        psum = ctx.enter_context(tc.psum_pool(name="psum", bufs=1))
+        ctx.enter_context(tc.manual_schedule())
+
+        ident = keep.tile([P, P], F32, name="ident")
+        scale = keep.tile([P, HIDDEN], F32, name="scale")
+        fc2_words = keep.tile([P, 2 * 2 * CHANNELS], U8, name="fc2_words", align_bytes=64)
+        fc2_scales = keep.tile([P, 2 * CHANNELS], U8, name="fc2_scales", align_bytes=64)
+        head_words = keep.tile([P, 2 * 2 * OUT], U8, name="head_words", align_bytes=64)
+        head_scales = keep.tile([P, 2 * OUT], U8, name="head_scales", align_bytes=64)
+        head_bias = keep.tile([P, OUT], BF16, name="head_bias")
+        bias_rows = keep.tile([P, P], BF16, name="bias_rows")
+        bias_rows32 = keep.tile([P, P], F32, name="bias_rows32")
+        bias = keep.tile([P, 8], F32, name="bias")
+        bias_less = keep.tile([P, 8], F32, name="bias_less")
+        one = keep.tile([P, 1], F32, name="one")
+        junk = keep.tile([P, 1], F32, name="junk")
+
+        nc.vector.memset(one[:], 1.0)
+        nc.scalar.dma_start(out=scale[:], in_=hdn_scale.rearrange("a o k -> (a o k)").partition_broadcast(P))
+        nc.scalar.activation(out=junk[:], in_=one[:], func=ACT.Ln)
+        make_identity(nc, ident[:])
+        nc.vector.memset(fc2_scales[:].bitcast(I32), 0)
+        nc.vector.memset(bias_rows[:], 0.0)
+        nc.gpsimd.memset(head_scales[:].bitcast(I32), 0)
+
+        xb = {}
+
+        def load(s, pieces):
+            xb[s] = work.tile([P, 4 * HIDDEN], U8, name="xb", bufs=6)
+            n = 4 // pieces
+            for q in range(pieces):
+                nc.sync.dma_start(
+                    out=xb[s][:, q * n * HIDDEN : (q + 1) * n * HIDDEN],
+                    in_=hdn_bytes[:, 4 * s + q * n : 4 * s + (q + 1) * n, :].rearrange("b i k -> b (i k)"),
+                )
+
+        load(0, 4)
+        nc.sync.dma_start(
+            out=fc2_words[:].rearrange("p (g b) -> p g b", g=2), in_=fc2_w_words.rearrange("g p b -> p g b")
+        )
+        for q in range(4):
+            nc.sync.dma_start(
+                out=fc2_scales[32 * q : 32 * q + 4, :].bitcast(I32).rearrange("q (g n) -> q g n", g=2),
+                in_=fc2_w_scales[:, 4 * q : 4 * q + 4, :].bitcast(I32).rearrange("g q n -> q g n"),
+            )
+        nc.sync.dma_start(out=bias_rows[0:8, :], in_=fc2_b.rearrange("(j c) -> j c", j=8))
+        for s in range(1, 4):
+            load(s, 1)
+
+        rbank = [psum.tile([P, 512], F32, name="rbank%d" % h, tag="r%d" % h) for h in range(2)]
+        xw, xt, grp, codes, csc, tok, y, sq, cube = {}, {}, {}, {}, {}, {}, {}, {}, {}
+
+        def widen(i):
+            xw[i] = work.tile([P, HIDDEN], BF16, name="xw", bufs=6, align_bytes=64)
+            q = i % 4
+            nc.vector.tensor_tensor(
+                out=xw[i][:], in0=xb[i // 4][:, q * HIDDEN : (q + 1) * HIDDEN].bitcast(FP8), in1=scale[:], op=ALU.mult
+            )
+
+        def turn(i):
+            xt[i] = psum.tile([P, 4, P], F32, name="xt", tag="x%d" % (i % 2))
+            words = xw[i][:].bitcast(F32)
+            for g in range(2):
+                for u in range(2):
+                    nc.tensor.transpose(xt[i][:, 2 * g + u, :], words[:, 256 * g + u : 256 * (g + 1) : 2], ident[:])
+
+        def empty(i):
+            s = i // 4
+            if i % 4 == 0:
+                grp[s] = work.tile([P, 4 * HIDDEN], BF16, name="grp", bufs=2, align_bytes=64)
+            view = grp[s][:].bitcast(F32).rearrange("p (g i b u) -> p g i b u", g=2, i=4, b=P)
+            nc.scalar.copy(out=view[:, :, i % 4, :, :], in_=xt[i][:].rearrange("p (g u) b -> p g b u", g=2))
+
+        def quantize(s):
+            codes[s] = work.tile([P, 1024], U32, name="codes", bufs=3, align_bytes=64)
+            csc[s] = work.tile([P, 1024], U8, name="csc", bufs=3, align_bytes=64)
+            nc.vector.quantize_mx(out=codes[s][:].bitcast(FP8X4), scales=csc[s][:], in_=grp[s][:])
+
+        def multiply(u):
+            s, h = divmod(u, 2)
+            for j in range(4):
+                tok[u, j] = psum.tile([P, 512], F32, name="tok", tag="t%d" % j)
+                c0 = (4 * h + j) * P
+                for g in range(2):
+                    col = g * CHANNELS + c0
+                    nc.tensor.matmul_mx(
+                        out=tok[u, j][:],
+                        lhsT=fc2_words[:, 2 * col : 2 * col + 256].bitcast(FP4X4),
+                        lhsT_scale=fc2_scales[:, col : col + P],
+                        rhs=codes[s][:, 512 * g : 512 * (g + 1)].bitcast(FP8X4),
+                        rhs_scale=csc[s][:, 512 * g : 512 * (g + 1)],
+                        start=(g == 0),
+                        stop=(g == 1),
+                    )
+
+        def clipped_late(u, j):
+            return j == 3
+
+        def first_scalar(u):
+            h = u % 2
+            for pair in range(2):
+                y[u, pair] = work.tile([P, 1024], F32, name="y", bufs=3)
+                sq[u, pair] = work.tile([P, 1024], F32, name="sq", bufs=4)
+            for j in range(4):
+                c = 4 * h + j
+                if clipped_late(u, j):
+                    nc.scalar.activation(
+                        out=sq[u, j // 2][:, 512 * (j % 2) : 512 * (j % 2) + 512], in_=tok[u, j][:],
+                        func=ACT.Square, bias=bias[:, c : c + 1],
+                    )
+                else:
+                    nc.scalar.activation(
+                        out=y[u, j // 2][:, 512 * (j % 2) : 512 * (j % 2) + 512], in_=tok[u, j][:],
+                        func=ACT.Relu, bias=bias_less[:, c : c + 1],
+                    )
+
+        def groups(u):
+            res = []
+            for pair in range(2):
+                js = [j for j in (2 * pair, 2 * pair + 1) if not clipped_late(u, j)]
+                if js:
+                    res.append((pair, 512 * (js[0] % 2), 512 * len(js)))
+            return res
+
+        def second_scalar(u):
+            for pair, a, w in groups(u):
+                nc.scalar.activation(
+                    out=sq[u, pair][:, a : a + w], in_=y[u, pair][:, a : a + w], func=ACT.Square, bias=EPS
+                )
+
+        def cubes(u):
+            h = u % 2
+            for pair in range(2):
+                cube[u, pair] = work.tile([P, 1024], F32, name="cube", bufs=6)
+            late = [j for j in range(4) if clipped_late(u, j)]
+            for j in late:
+                c = 4 * h + j
+                cols = slice(512 * (j % 2), 512 * (j % 2) + 512)
+                nc.vector.scalar_tensor_tensor(
+                    out=cube[u, j // 2][:, cols], in0=tok[u, j][:], scalar=bias[:, c : c + 1],
+                    in1=sq[u, j // 2][:, cols], op0=ALU.add, op1=ALU.mult,
+                )
+            for n, (pair, a, w) in enumerate(groups(u)):
+                nc.vector.scalar_tensor_tensor(
+                    out=cube[u, pair][:, a : a + w], in0=y[u, pair][:, a : a + w], scalar=EPS,
+                    in1=sq[u, pair][:, a : a + w], op0=ALU.add, op1=ALU.mult,
+                )
+                if n == 0:
+                    for j in late:
+                        cols = slice(512 * (j % 2), 512 * (j % 2) + 512)
+                        nc.vector.tensor_scalar(
+                            out=cube[u, j // 2][:, cols], in0=cube[u, j // 2][:, cols],
+                            scalar1=EPS_CUBE, scalar2=None, op0=ALU.max,
+                        )
+
+        def pool(u):
+            s, h = divmod(u, 2)
+            for j in range(4):
+                for i in range(4):
+                    a = 512 * (j % 2) + P * i
+                    nc.tensor.matmul(
+                        out=rbank[h][:, P * j : P * j + P], lhsT=cube[u, j // 2][:, a : a + P], rhs=ident[:],
+                        is_transpose=True, start=(s == 0 and j == 0 and i == 0),
+                        stop=(s == STEPS - 1 and j == 3 and i == 3),
+                    )
+
+        def prepare_bias():
+            nc.vector.tensor_copy(out=bias_rows32[:], in_=bias_rows[:])
+            turned = psum.tile([P, P], F32, name="turned", tag="t0")
+            nc.tensor.transpose(turned[:], bias_rows32[:], ident[:])
+            nc.vector.tensor_copy(out=bias[:], in_=turned[:, 0:8])
+            nc.vector.tensor_scalar(out=bias_less[:], in0=bias[:], scalar1=-EPS, scalar2=None, op0=ALU.add)
+
+        for k in range(UNITS + 5):
+            u = k - 4
+            if k >= 1 and k + 3 < STEPS:
+                load(k + 3, 1)
+            if k == 5:
+                nc.sync.dma_start(
+                    out=head_words[:].bitcast(I32).rearrange("p (g b) -> p g b", g=2),
+                    in_=head_w_words.bitcast(I32).rearrange("g p b -> p g b"),
+                )
+                for q in range(4):
+                    nc.sync.dma_start(
+                        out=head_scales[32 * q : 32 * q + 4, :].bitcast(I32).rearrange("q (g n) -> q g n", g=2),
+                        in_=head_w_scales[:, 4 * q : 4 * q + 4, :].bitcast(I32).rearrange("g q n -> q g n"),
+                    )
+                nc.sync.dma_start(out=head_bias[:], in_=head_b.partition_broadcast(P))
+            if 0 <= u < UNITS:
+                multiply(u)
+            for i in (2 * k, 2 * k + 1):
+                if i < TOKENS:
+                    widen(i)
+            if k == 2:
+                prepare_bias()
+            turned_now = [i for i in (2 * k - 2, 2 * k - 1) if 0 <= i < TOKENS]
+            for i in turned_now:
+                turn(i)
+            if 0 <= u - 1 < UNITS:
+                pool(u - 1)
+            if 0 <= u < UNITS:
+                first_scalar(u)
+            for i in turned_now:
+                empty(i)
+            if 0 <= u < UNITS:
+                second_scalar(u)
+                cubes(u)
+            if k % 2 == 0 and 0 <= k // 2 - 1 < STEPS:
+                quantize(k // 2 - 1)
+
+        logs = keep.tile([P, CHANNELS], F32, name="logs")
+        g_bf = keep.tile([P, CHANNELS], BF16, name="g_bf", align_bytes=64)
+        g_grp = keep.tile([P, CHANNELS], BF16, name="g_grp", align_bytes=64)
+        g_codes = keep.tile([P, 2 * P], U32, name="g_codes", align_bytes=64)
+        g_scales = keep.tile([P, 2 * P], U8, name="g_scales", align_bytes=64)
+        d = keep.tile([P, OUT], F32, name="d")
+        res = keep.tile([P, OUT], F32, name="res")
+        waste = keep.tile([P, 512], F32, name="waste")
+        parts = keep.tile([P, 8], F32, name="parts")
+        total = keep.tile([P, 1], F32, name="total")
+        clipped = keep.tile([P, 1], F32, name="clipped")
+        norm = keep.tile([P, 1], F32, name="norm")
+        inv = keep.tile([P, 1], F32, name="inv")
+
+        for h in range(2):
+            nc.scalar.activation(
+                out=logs[:, 512 * h : 512 * h + 512], in_=rbank[h][:], func=ACT.Ln, scale=1.0 / TOKENS
+            )
+        for h in range(2):
+            nc.scalar.activation(
+                out=g_bf[:, 512 * h : 512 * h + 512], in_=logs[:, 512 * h : 512 * h + 512], func=ACT.Exp,
+                scale=1.0 / 3.0,
+            )
+        nc.scalar.activation(out=junk[:], in_=one[:], func=ACT.Sqrt)
+        for h in range(2):
+            gt = psum.tile([P, 2, P], F32, name="gt", tag="x%d" % h)
+            words = g_bf[:].bitcast(F32)
+            for u in range(2):
+                nc.tensor.transpose(gt[:, u, :], words[:, 256 * h + u : 256 * (h + 1) : 2], ident[:])
+            cols = slice(512 * h, 512 * h + 512)
+            nc.vector.tensor_copy(
+                out=g_grp[:, cols].bitcast(F32).rearrange("p (b u) -> p b u", u=2),
+                in_=gt[:].rearrange("p u b -> p b u"),
+            )
+            nc.vector.quantize_mx(
+                out=g_codes[:, P * h : P * h + P].bitcast(FP8X4), scales=g_scales[:, P * h : P * h + P],
+                in_=g_grp[:, cols],
+            )
+        tags = ["t0", "t1", "t2", "t3", "r0", "r1", "x0", "x1"]
+        acc = [psum.tile([P, 512], F32, name="acc%d" % n, tag=tags[n]) for n in range(8)]
+
+        def head(n, g):
+            col = g * OUT + 512 * n
+            nc.tensor.matmul_mx(
+                out=acc[n][:],
+                lhsT=g_codes[:, P * g : P * g + P].bitcast(FP8X4),
+                lhsT_scale=g_scales[:, P * g : P * g + P],
+                rhs=head_words[:, 2 * col : 2 * col + 1024].bitcast(FP4X4),
+                rhs_scale=head_scales[:, col : col + 512],
+                start=(g == 0),
+                stop=(g == 1),
+            )
+
+        for n in range(4):
+            head(n, 0)
+        for n in range(4):
+            head(n, 1)
+        for n in range(4, 8):
+            head(n, 0)
+            head(n, 1)
+        for n in range(8):
+            cols = slice(512 * n, 512 * n + 512)
+            nc.vector.tensor_tensor(out=d[:, cols], in0=acc[n][:], in1=head_bias[:, cols], op=ALU.add)
+            nc.scalar.activation(out=waste[:], in_=d[:, cols], func=ACT.Square, accum_out=parts[:, n : n + 1])
+        nc.vector.tensor_reduce(out=total[:], in_=parts[:], axis=AX.X, op=ALU.add)
+        nc.vector.tensor_scalar(out=clipped[:], in0=total[:], scalar1=1e-24, scalar2=None, op0=ALU.max)
+        nc.scalar.activation(out=norm[:], in_=clipped[:], func=ACT.Sqrt)
+        nc.vector.reciprocal(out=inv[:], in_=norm[:])
+        for n in (0, 1, 2, 3, 4, 5, 6, 7):
+            cols = slice(512 * n, 512 * n + 512)
+            if n in (2, 3):
+                nc.scalar.activation(out=res[:, cols], in_=d[:, cols], func=ACT.Copy, scale=inv[:, 0:1])
+            else:
+                nc.vector.tensor_scalar(
+                    out=res[:, cols], in0=d[:, cols], scalar1=inv[:, 0:1], scalar2=None, op0=ALU.mult
+                )
+        for n in (0, 4, 2, 6):
+            cols = slice(512 * n, 512 * n + 1024)
+            nc.sync.dma_start(out=out[:, cols], in_=res[:, cols])

@@ -16,13 +16,11 @@ FP8X4 = mybir.dt.float8_e4m3fn_x4
 FP4X4 = mybir.dt.float4_e2m1fn_x4
 ALU = mybir.AluOpType
 ACT = mybir.ActivationFunctionType
-AX = mybir.AxisListType
 
 P = 128
 EPS = 1e-6
 EPS_CUBE = 1e-18
 STEPS = 9
-UNITS = 18
 
 
 def tile_tokenmudule_pb_w4_kernel(
@@ -110,15 +108,15 @@ def tile_tokenmudule_pb_w4_kernel(
             csc[s] = work.tile([P, 1024], U8, name="csc", bufs=3, align_bytes=64)
             nc.vector.quantize_mx(out=codes[s][:].bitcast(FP8X4), scales=csc[s][:], in_=grp[s][:])
 
-        def multiply(u):
-            s, h = divmod(u, 2)
-            for j in range(4):
-                tok[u, j] = psum.tile([P, 512], F32, name="tok", tag="t%d" % j)
-                c0 = (4 * h + j) * P
+        def multiply(w):
+            s = w // 4
+            for e in range(2):
+                tok[w, e] = psum.tile([P, 512], F32, name="tok", tag="t%d" % (2 * (w % 2) + e))
+                c0 = (2 * (w % 4) + e) * P
                 for g in range(2):
                     col = g * CHANNELS + c0
                     nc.tensor.matmul_mx(
-                        out=tok[u, j][:],
+                        out=tok[w, e][:],
                         lhsT=fc2_words[:, 2 * col : 2 * col + 256].bitcast(FP4X4),
                         lhsT_scale=fc2_scales[:, col : col + P],
                         rhs=codes[s][:, 512 * g : 512 * (g + 1)].bitcast(FP8X4),
@@ -127,75 +125,56 @@ def tile_tokenmudule_pb_w4_kernel(
                         stop=(g == 1),
                     )
 
-        def clipped_late(u, j):
-            return j == 3
+        def clipped_late(w):
+            return w >= 30 or w % 2 == 1
 
-        def first_scalar(u):
-            h = u % 2
-            for pair in range(2):
-                y[u, pair] = work.tile([P, 1024], F32, name="y", bufs=3)
-                sq[u, pair] = work.tile([P, 1024], F32, name="sq", bufs=4)
-            for j in range(4):
-                c = 4 * h + j
-                if clipped_late(u, j):
+        def first_scalar(w):
+            y[w] = work.tile([P, 1024], F32, name="y", bufs=3)
+            sq[w] = work.tile([P, 1024], F32, name="sq", bufs=4)
+            for e in range(2):
+                c = 2 * (w % 4) + e
+                half = slice(512 * e, 512 * e + 512)
+                if e == 1 and clipped_late(w):
                     nc.scalar.activation(
-                        out=sq[u, j // 2][:, 512 * (j % 2) : 512 * (j % 2) + 512], in_=tok[u, j][:],
-                        func=ACT.Square, bias=bias[:, c : c + 1],
+                        out=sq[w][:, half], in_=tok[w, e][:], func=ACT.Square, bias=bias[:, c : c + 1]
                     )
                 else:
                     nc.scalar.activation(
-                        out=y[u, j // 2][:, 512 * (j % 2) : 512 * (j % 2) + 512], in_=tok[u, j][:],
-                        func=ACT.Relu, bias=bias_less[:, c : c + 1],
+                        out=y[w][:, half], in_=tok[w, e][:], func=ACT.Relu, bias=bias_less[:, c : c + 1]
                     )
 
-        def groups(u):
-            res = []
-            for pair in range(2):
-                js = [j for j in (2 * pair, 2 * pair + 1) if not clipped_late(u, j)]
-                if js:
-                    res.append((pair, 512 * (js[0] % 2), 512 * len(js)))
-            return res
+        def second_scalar(w):
+            n = 512 if clipped_late(w) else 1024
+            nc.scalar.activation(out=sq[w][:, 0:n], in_=y[w][:, 0:n], func=ACT.Square, bias=EPS)
 
-        def second_scalar(u):
-            for pair, a, w in groups(u):
-                nc.scalar.activation(
-                    out=sq[u, pair][:, a : a + w], in_=y[u, pair][:, a : a + w], func=ACT.Square, bias=EPS
-                )
-
-        def cubes(u):
-            h = u % 2
-            for pair in range(2):
-                cube[u, pair] = work.tile([P, 1024], F32, name="cube", bufs=6)
-            late = [j for j in range(4) if clipped_late(u, j)]
-            for j in late:
-                c = 4 * h + j
-                cols = slice(512 * (j % 2), 512 * (j % 2) + 512)
+        def cubes(w):
+            cube[w] = work.tile([P, 1024], F32, name="cube", bufs=5)
+            late = clipped_late(w)
+            n = 512 if late else 1024
+            if late:
+                c = 2 * (w % 4) + 1
                 nc.vector.scalar_tensor_tensor(
-                    out=cube[u, j // 2][:, cols], in0=tok[u, j][:], scalar=bias[:, c : c + 1],
-                    in1=sq[u, j // 2][:, cols], op0=ALU.add, op1=ALU.mult,
+                    out=cube[w][:, 512:1024], in0=tok[w, 1][:], scalar=bias[:, c : c + 1],
+                    in1=sq[w][:, 512:1024], op0=ALU.add, op1=ALU.mult,
                 )
-            for n, (pair, a, w) in enumerate(groups(u)):
-                nc.vector.scalar_tensor_tensor(
-                    out=cube[u, pair][:, a : a + w], in0=y[u, pair][:, a : a + w], scalar=EPS,
-                    in1=sq[u, pair][:, a : a + w], op0=ALU.add, op1=ALU.mult,
+            nc.vector.scalar_tensor_tensor(
+                out=cube[w][:, 0:n], in0=y[w][:, 0:n], scalar=EPS, in1=sq[w][:, 0:n], op0=ALU.add, op1=ALU.mult
+            )
+            if late:
+                nc.vector.tensor_scalar(
+                    out=cube[w][:, 512:1024], in0=cube[w][:, 512:1024], scalar1=EPS_CUBE, scalar2=None, op0=ALU.max
                 )
-                if n == 0:
-                    for j in late:
-                        cols = slice(512 * (j % 2), 512 * (j % 2) + 512)
-                        nc.vector.tensor_scalar(
-                            out=cube[u, j // 2][:, cols], in0=cube[u, j // 2][:, cols],
-                            scalar1=EPS_CUBE, scalar2=None, op0=ALU.max,
-                        )
 
-        def pool(u):
-            s, h = divmod(u, 2)
-            for j in range(4):
+        def pool(w):
+            for e in range(2):
+                j = 2 * (w % 4) + e
+                h, jj = divmod(j, 4)
                 for i in range(4):
-                    a = 512 * (j % 2) + P * i
+                    a = 512 * e + P * i
                     nc.tensor.matmul(
-                        out=rbank[h][:, P * j : P * j + P], lhsT=cube[u, j // 2][:, a : a + P], rhs=ident[:],
-                        is_transpose=True, start=(s == 0 and j == 0 and i == 0),
-                        stop=(s == STEPS - 1 and j == 3 and i == 3),
+                        out=rbank[h][:, P * jj : P * jj + P], lhsT=cube[w][:, a : a + P], rhs=ident[:],
+                        is_transpose=True, start=(w < 4 and jj == 0 and i == 0),
+                        stop=(w >= 32 and jj == 3 and i == 3),
                     )
 
         def prepare_bias():
@@ -205,11 +184,12 @@ def tile_tokenmudule_pb_w4_kernel(
             nc.vector.tensor_copy(out=bias[:], in_=turned[:, 0:8])
             nc.vector.tensor_scalar(out=bias_less[:], in0=bias[:], scalar1=-EPS, scalar2=None, op0=ALU.add)
 
-        for k in range(UNITS + 5):
-            u = k - 4
-            if k >= 1 and k + 3 < STEPS:
-                load(k + 3, 1)
-            if k == 5:
+        pairs = 4 * STEPS
+        for k in range(pairs + 9):
+            w = k - 7
+            if k % 2 == 0 and 4 <= k // 2 + 3 < STEPS:
+                load(k // 2 + 3, 1)
+            if k == 12:
                 nc.sync.dma_start(
                     out=head_words[:].bitcast(I32).rearrange("p (g b) -> p g b", g=2),
                     in_=head_w_words.bitcast(I32).rearrange("g p b -> p g b"),
@@ -220,27 +200,25 @@ def tile_tokenmudule_pb_w4_kernel(
                         in_=head_w_scales[:, 4 * q : 4 * q + 4, :].bitcast(I32).rearrange("g q n -> q g n"),
                     )
                 nc.sync.dma_start(out=head_bias[:], in_=head_b.partition_broadcast(P))
-            if 0 <= u < UNITS:
-                multiply(u)
-            for i in (2 * k, 2 * k + 1):
-                if i < TOKENS:
-                    widen(i)
-            if k == 2:
+            if k < TOKENS:
+                widen(k)
+            if k == 5:
                 prepare_bias()
-            turned_now = [i for i in (2 * k - 2, 2 * k - 1) if 0 <= i < TOKENS]
-            for i in turned_now:
-                turn(i)
-            if 0 <= u - 1 < UNITS:
-                pool(u - 1)
-            if 0 <= u < UNITS:
-                first_scalar(u)
-            for i in turned_now:
-                empty(i)
-            if 0 <= u < UNITS:
-                second_scalar(u)
-                cubes(u)
-            if k % 2 == 0 and 0 <= k // 2 - 1 < STEPS:
-                quantize(k // 2 - 1)
+            if 0 <= w < pairs:
+                multiply(w)
+            if 0 <= k - 1 < TOKENS:
+                turn(k - 1)
+            if 0 <= w - 2 < pairs:
+                pool(w - 2)
+            if 0 <= w < pairs:
+                first_scalar(w)
+                second_scalar(w)
+            if 0 <= k - 1 < TOKENS:
+                empty(k - 1)
+            if 0 <= w - 1 < pairs:
+                cubes(w - 1)
+            if k % 4 == 1 and 0 <= (k - 5) // 4 < STEPS:
+                quantize((k - 5) // 4)
 
         logs = keep.tile([P, CHANNELS], F32, name="logs")
         g_bf = keep.tile([P, CHANNELS], BF16, name="g_bf", align_bytes=64)
@@ -252,7 +230,8 @@ def tile_tokenmudule_pb_w4_kernel(
         waste = keep.tile([P, 512], F32, name="waste")
         parts = keep.tile([P, 8], F32, name="parts")
         total = keep.tile([P, 1], F32, name="total")
-        clipped = keep.tile([P, 1], F32, name="clipped")
+        eight = keep.tile([P, 8], F32, name="eight")
+        floored = keep.tile([P, 1], F32, name="floored")
         norm = keep.tile([P, 1], F32, name="norm")
         inv = keep.tile([P, 1], F32, name="inv")
 
@@ -266,6 +245,9 @@ def tile_tokenmudule_pb_w4_kernel(
                 scale=1.0 / 3.0,
             )
         nc.scalar.activation(out=junk[:], in_=one[:], func=ACT.Sqrt)
+        warm = psum.tile([P, 512], F32, name="warm", tag="t0")
+        for n in range(10):
+            nc.tensor.matmul(warm[:], lhsT=bias_rows[:], rhs=head_bias[:, 0:512], start=True, stop=True)
         for h in range(2):
             gt = psum.tile([P, 2, P], F32, name="gt", tag="x%d" % h)
             words = g_bf[:].bitcast(F32)
@@ -306,10 +288,10 @@ def tile_tokenmudule_pb_w4_kernel(
             cols = slice(512 * n, 512 * n + 512)
             nc.vector.tensor_tensor(out=d[:, cols], in0=acc[n][:], in1=head_bias[:, cols], op=ALU.add)
             nc.scalar.activation(out=waste[:], in_=d[:, cols], func=ACT.Square, accum_out=parts[:, n : n + 1])
-        nc.vector.tensor_reduce(out=total[:], in_=parts[:], axis=AX.X, op=ALU.add)
-        nc.vector.tensor_scalar(out=clipped[:], in0=total[:], scalar1=1e-24, scalar2=None, op0=ALU.max)
-        nc.scalar.activation(out=norm[:], in_=clipped[:], func=ACT.Sqrt)
-        nc.vector.reciprocal(out=inv[:], in_=norm[:])
+        nc.scalar.activation(out=eight[:], in_=parts[:], func=ACT.Copy, accum_out=total[:])
+        nc.scalar.activation(out=norm[:], in_=total[:], func=ACT.Sqrt, bias=2.0**-110)
+        nc.vector.tensor_scalar(out=floored[:], in0=norm[:], scalar1=1e-12, scalar2=None, op0=ALU.max)
+        nc.vector.reciprocal(out=inv[:], in_=floored[:])
         for n in (0, 1, 2, 3, 4, 5, 6, 7):
             cols = slice(512 * n, 512 * n + 512)
             if n in (2, 3):

@@ -21,6 +21,7 @@ P = 128
 EPS = 1e-6
 EPS_CUBE = 1e-18
 STEPS = 9
+EARLY = 4
 
 
 def tile_tokenmudule_pb_w4_kernel(
@@ -35,6 +36,7 @@ def tile_tokenmudule_pb_w4_kernel(
 
         ident = keep.tile([P, P], F32, name="ident")
         scale = keep.tile([P, HIDDEN], F32, name="scale")
+        scale_turned = keep.tile([P, 8], F32, name="scale_turned")
         fc2_words = keep.tile([P, 2 * 2 * CHANNELS], U8, name="fc2_words", align_bytes=64)
         fc2_scales = keep.tile([P, 2 * CHANNELS], U8, name="fc2_scales", align_bytes=64)
         head_words = keep.tile([P, 2 * 2 * OUT], U8, name="head_words", align_bytes=64)
@@ -44,15 +46,20 @@ def tile_tokenmudule_pb_w4_kernel(
         bias_rows32 = keep.tile([P, P], F32, name="bias_rows32")
         bias = keep.tile([P, 8], F32, name="bias")
         bias_less = keep.tile([P, 8], F32, name="bias_less")
+        quiet = keep.tile([P, 512], BF16, name="quiet")
         one = keep.tile([P, 1], F32, name="one")
         junk = keep.tile([P, 1], F32, name="junk")
 
         nc.vector.memset(one[:], 1.0)
-        nc.scalar.dma_start(out=scale[:], in_=hdn_scale.rearrange("a o k -> (a o k)").partition_broadcast(P))
+        nc.scalar.dma_start(
+            out=scale_turned[:].rearrange("p (g t) -> p g t", g=2),
+            in_=hdn_scale.rearrange("a o (g p t) -> p (a o g) t", g=2, p=P),
+        )
         nc.scalar.activation(out=junk[:], in_=one[:], func=ACT.Ln)
         make_identity(nc, ident[:])
         nc.vector.memset(fc2_scales[:].bitcast(I32), 0)
         nc.vector.memset(bias_rows[:], 0.0)
+        nc.gpsimd.memset(quiet[:], 0.0)
         nc.gpsimd.memset(head_scales[:].bitcast(I32), 0)
 
         xb = {}
@@ -67,6 +74,8 @@ def tile_tokenmudule_pb_w4_kernel(
                 )
 
         load(0, 4)
+        load(1, 1)
+        nc.sync.dma_start(out=scale[:], in_=hdn_scale.rearrange("a o k -> (a o k)").partition_broadcast(P))
         nc.sync.dma_start(
             out=fc2_words[:].rearrange("p (g b) -> p g b", g=2), in_=fc2_w_words.rearrange("g p b -> p g b")
         )
@@ -76,7 +85,7 @@ def tile_tokenmudule_pb_w4_kernel(
                 in_=fc2_w_scales[:, 4 * q : 4 * q + 4, :].bitcast(I32).rearrange("g q n -> q g n"),
             )
         nc.sync.dma_start(out=bias_rows[0:8, :], in_=fc2_b.rearrange("(j c) -> j c", j=8))
-        for s in range(1, 4):
+        for s in range(2, 4):
             load(s, 1)
 
         rbank = [psum.tile([P, 512], F32, name="rbank%d" % h, tag="r%d" % h) for h in range(2)]
@@ -85,9 +94,15 @@ def tile_tokenmudule_pb_w4_kernel(
         def widen(i):
             xw[i] = work.tile([P, HIDDEN], BF16, name="xw", bufs=6, align_bytes=64)
             q = i % 4
-            nc.vector.tensor_tensor(
-                out=xw[i][:], in0=xb[i // 4][:, q * HIDDEN : (q + 1) * HIDDEN].bitcast(FP8), in1=scale[:], op=ALU.mult
-            )
+            values = xb[i // 4][:, q * HIDDEN : (q + 1) * HIDDEN].bitcast(FP8)
+            if i == 0:
+                for g in range(2):
+                    half = slice(512 * g, 512 * g + 512)
+                    nc.scalar.copy(out=xw[i][:, half], in_=values[:, half])
+            elif i < EARLY:
+                nc.scalar.copy(out=xw[i][:], in_=values)
+            else:
+                nc.vector.tensor_tensor(out=xw[i][:], in0=values, in1=scale[:], op=ALU.mult)
 
         def turn(i):
             xt[i] = psum.tile([P, 4, P], F32, name="xt", tag="x%d" % (i % 2))
@@ -100,6 +115,18 @@ def tile_tokenmudule_pb_w4_kernel(
             s = i // 4
             if i % 4 == 0:
                 grp[s] = work.tile([P, 4 * HIDDEN], BF16, name="grp", bufs=2, align_bytes=64)
+            if i < EARLY:
+                rows = grp[s][:].rearrange("p (g i b u e) -> p g i b u e", g=2, i=4, b=P, u=2)
+                for g in range(2):
+                    nc.vector.tensor_tensor(
+                        out=rows[:, g, i % 4, :, :, :],
+                        in0=xt[i][:, 2 * g : 2 * g + 2, :].bitcast(BF16).rearrange("p u (b e) -> p b u e", e=2),
+                        in1=scale_turned[:, 4 * g : 4 * g + 4]
+                        .rearrange("p (o u e) -> p o u e", o=1, u=2)
+                        .to_broadcast([P, P, 2, 2]),
+                        op=ALU.mult,
+                    )
+                return
             view = grp[s][:].bitcast(F32).rearrange("p (g i b u) -> p g i b u", g=2, i=4, b=P)
             nc.scalar.copy(out=view[:, :, i % 4, :, :], in_=xt[i][:].rearrange("p (g u) b -> p g b u", g=2))
 
@@ -125,45 +152,59 @@ def tile_tokenmudule_pb_w4_kernel(
                         stop=(g == 1),
                     )
 
-        def clipped_late(w):
-            return w >= 30 or w % 2 == 1
+        def late(w):
+            if w >= 34:
+                return (0, 1)
+            return (1,) if w >= 28 or w % 2 == 1 else ()
+
+        def half(e):
+            return slice(512 * e, 512 * e + 512)
 
         def first_scalar(w):
-            y[w] = work.tile([P, 1024], F32, name="y", bufs=3)
-            sq[w] = work.tile([P, 1024], F32, name="sq", bufs=4)
+            y[w] = work.tile([P, 1024], F32, name="y", bufs=5)
+            sq[w] = work.tile([P, 1024], F32, name="sq", bufs=5)
             for e in range(2):
                 c = 2 * (w % 4) + e
-                half = slice(512 * e, 512 * e + 512)
-                if e == 1 and clipped_late(w):
+                if e in late(w):
                     nc.scalar.activation(
-                        out=sq[w][:, half], in_=tok[w, e][:], func=ACT.Square, bias=bias[:, c : c + 1]
+                        out=sq[w][:, half(e)], in_=tok[w, e][:], func=ACT.Square, bias=bias[:, c : c + 1]
                     )
                 else:
                     nc.scalar.activation(
-                        out=y[w][:, half], in_=tok[w, e][:], func=ACT.Relu, bias=bias_less[:, c : c + 1]
+                        out=y[w][:, half(e)], in_=tok[w, e][:], func=ACT.Relu, bias=bias_less[:, c : c + 1]
                     )
 
         def second_scalar(w):
-            n = 512 if clipped_late(w) else 1024
-            nc.scalar.activation(out=sq[w][:, 0:n], in_=y[w][:, 0:n], func=ACT.Square, bias=EPS)
+            n = 1024 - 512 * len(late(w))
+            if n:
+                nc.scalar.activation(out=sq[w][:, 0:n], in_=y[w][:, 0:n], func=ACT.Square, bias=EPS)
 
-        def cubes(w):
-            cube[w] = work.tile([P, 1024], F32, name="cube", bufs=5)
-            late = clipped_late(w)
-            n = 512 if late else 1024
-            if late:
-                c = 2 * (w % 4) + 1
+        def late_product(w):
+            cube[w] = work.tile([P, 1024], F32, name="cube", bufs=6)
+            for e in late(w):
+                c = 2 * (w % 4) + e
                 nc.vector.scalar_tensor_tensor(
-                    out=cube[w][:, 512:1024], in0=tok[w, 1][:], scalar=bias[:, c : c + 1],
-                    in1=sq[w][:, 512:1024], op0=ALU.add, op1=ALU.mult,
+                    out=cube[w][:, half(e)], in0=tok[w, e][:], scalar=bias[:, c : c + 1],
+                    in1=sq[w][:, half(e)], op0=ALU.add, op1=ALU.mult,
                 )
-            nc.vector.scalar_tensor_tensor(
-                out=cube[w][:, 0:n], in0=y[w][:, 0:n], scalar=EPS, in1=sq[w][:, 0:n], op0=ALU.add, op1=ALU.mult
-            )
-            if late:
+
+        def late_clip(w):
+            for e in late(w):
                 nc.vector.tensor_scalar(
-                    out=cube[w][:, 512:1024], in0=cube[w][:, 512:1024], scalar1=EPS_CUBE, scalar2=None, op0=ALU.max
+                    out=cube[w][:, half(e)], in0=cube[w][:, half(e)], scalar1=EPS_CUBE, scalar2=None, op0=ALU.max
                 )
+
+        def product(w):
+            n = 1024 - 512 * len(late(w))
+            if n:
+                nc.vector.scalar_tensor_tensor(
+                    out=cube[w][:, 0:n], in0=y[w][:, 0:n], scalar=EPS, in1=sq[w][:, 0:n], op0=ALU.add, op1=ALU.mult
+                )
+
+        def keep_warm(tag, count):
+            warm = psum.tile([P, 512], F32, name="warm", tag=tag)
+            for n in range(count):
+                nc.tensor.matmul(warm[:], lhsT=quiet[:, 0:P], rhs=quiet[:], start=True, stop=True)
 
         def pool(w):
             for e in range(2):
@@ -185,8 +226,8 @@ def tile_tokenmudule_pb_w4_kernel(
             nc.vector.tensor_scalar(out=bias_less[:], in0=bias[:], scalar1=-EPS, scalar2=None, op0=ALU.add)
 
         pairs = 4 * STEPS
-        for k in range(pairs + 9):
-            w = k - 7
+        for k in range(pairs + 13):
+            w = k - 8
             if k % 2 == 0 and 4 <= k // 2 + 3 < STEPS:
                 load(k // 2 + 3, 1)
             if k == 12:
@@ -200,25 +241,32 @@ def tile_tokenmudule_pb_w4_kernel(
                         in_=head_w_scales[:, 4 * q : 4 * q + 4, :].bitcast(I32).rearrange("g q n -> q g n"),
                     )
                 nc.sync.dma_start(out=head_bias[:], in_=head_b.partition_broadcast(P))
-            if k < TOKENS:
-                widen(k)
-            if k == 5:
+            if k == 6:
                 prepare_bias()
+            if k in (5, 6, 7):
+                keep_warm("t3", 3)
             if 0 <= w < pairs:
                 multiply(w)
-            if 0 <= k - 1 < TOKENS:
-                turn(k - 1)
-            if 0 <= w - 2 < pairs:
-                pool(w - 2)
+            if k % 4 == 2 and 0 <= (k - 6) // 4 < STEPS:
+                quantize((k - 6) // 4)
+            if k < TOKENS:
+                widen(k)
+            if 0 <= w - 4 < pairs:
+                pool(w - 4)
+            if 0 <= k - 2 < TOKENS:
+                turn(k - 2)
             if 0 <= w < pairs:
                 first_scalar(w)
-                second_scalar(w)
-            if 0 <= k - 1 < TOKENS:
-                empty(k - 1)
+            if 0 <= k - 2 < TOKENS:
+                empty(k - 2)
             if 0 <= w - 1 < pairs:
-                cubes(w - 1)
-            if k % 4 == 1 and 0 <= (k - 5) // 4 < STEPS:
-                quantize((k - 5) // 4)
+                second_scalar(w - 1)
+            if 0 <= w - 2 < pairs:
+                product(w - 2)
+            if 0 <= w - 1 < pairs:
+                late_clip(w - 1)
+            if 0 <= w < pairs:
+                late_product(w)
 
         logs = keep.tile([P, CHANNELS], F32, name="logs")
         g_bf = keep.tile([P, CHANNELS], BF16, name="g_bf", align_bytes=64)
@@ -229,8 +277,9 @@ def tile_tokenmudule_pb_w4_kernel(
         res = keep.tile([P, OUT], F32, name="res")
         waste = keep.tile([P, 512], F32, name="waste")
         parts = keep.tile([P, 8], F32, name="parts")
-        total = keep.tile([P, 1], F32, name="total")
-        eight = keep.tile([P, 8], F32, name="eight")
+        last_part = keep.tile([P, 1], F32, name="last_part")
+        seven = keep.tile([P, 1], F32, name="seven")
+        nc.gpsimd.memset(parts[:, 7:8], 2.0**-110)
         floored = keep.tile([P, 1], F32, name="floored")
         norm = keep.tile([P, 1], F32, name="norm")
         inv = keep.tile([P, 1], F32, name="inv")
@@ -245,14 +294,14 @@ def tile_tokenmudule_pb_w4_kernel(
                 scale=1.0 / 3.0,
             )
         nc.scalar.activation(out=junk[:], in_=one[:], func=ACT.Sqrt)
-        warm = psum.tile([P, 512], F32, name="warm", tag="t0")
-        for n in range(10):
-            nc.tensor.matmul(warm[:], lhsT=bias_rows[:], rhs=head_bias[:, 0:512], start=True, stop=True)
+        keep_warm("t0", 12)
         for h in range(2):
             gt = psum.tile([P, 2, P], F32, name="gt", tag="x%d" % h)
             words = g_bf[:].bitcast(F32)
             for u in range(2):
                 nc.tensor.transpose(gt[:, u, :], words[:, 256 * h + u : 256 * (h + 1) : 2], ident[:])
+            if h == 1:
+                keep_warm("t1", 2)
             cols = slice(512 * h, 512 * h + 512)
             nc.vector.tensor_copy(
                 out=g_grp[:, cols].bitcast(F32).rearrange("p (b u) -> p b u", u=2),
@@ -277,29 +326,27 @@ def tile_tokenmudule_pb_w4_kernel(
                 stop=(g == 1),
             )
 
-        for n in range(4):
-            head(n, 0)
-        for n in range(4):
-            head(n, 1)
-        for n in range(4, 8):
-            head(n, 0)
-            head(n, 1)
+        for n0 in range(0, 8, 2):
+            for g in range(2):
+                for n in (n0, n0 + 1):
+                    head(n, g)
         for n in range(8):
             cols = slice(512 * n, 512 * n + 512)
             nc.vector.tensor_tensor(out=d[:, cols], in0=acc[n][:], in1=head_bias[:, cols], op=ALU.add)
-            nc.scalar.activation(out=waste[:], in_=d[:, cols], func=ACT.Square, accum_out=parts[:, n : n + 1])
-        nc.scalar.activation(out=eight[:], in_=parts[:], func=ACT.Copy, accum_out=total[:])
-        nc.scalar.activation(out=norm[:], in_=total[:], func=ACT.Sqrt, bias=2.0**-110)
+            nc.scalar.activation(out=waste[:], in_=d[:, cols], func=ACT.Square, accum_out=last_part[:] if n == 7 else parts[:, n : n + 1])
+            if n == 7:
+                nc.vector.tensor_reduce(out=seven[:], in_=parts[:], axis=mybir.AxisListType.X, op=ALU.add)
+        nc.scalar.activation(out=norm[:], in_=last_part[:], func=ACT.Sqrt, bias=seven[:])
         nc.vector.tensor_scalar(out=floored[:], in0=norm[:], scalar1=1e-12, scalar2=None, op0=ALU.max)
         nc.vector.reciprocal(out=inv[:], in_=floored[:])
-        for n in (0, 1, 2, 3, 4, 5, 6, 7):
+        for n in range(8):
             cols = slice(512 * n, 512 * n + 512)
-            if n in (2, 3):
+            if n in (2, 5, 7):
                 nc.scalar.activation(out=res[:, cols], in_=d[:, cols], func=ACT.Copy, scale=inv[:, 0:1])
             else:
                 nc.vector.tensor_scalar(
                     out=res[:, cols], in0=d[:, cols], scalar1=inv[:, 0:1], scalar2=None, op0=ALU.mult
                 )
-        for n in (0, 4, 2, 6):
-            cols = slice(512 * n, 512 * n + 1024)
+        for n in (0, 2, 1, 3, 5, 4, 6, 7):
+            cols = slice(512 * n, 512 * n + 512)
             nc.sync.dma_start(out=out[:, cols], in_=res[:, cols])

@@ -74,8 +74,7 @@ def tile_tokenmudule_pb_w4_kernel(
                 )
 
         load(0, 4)
-        load(1, 1)
-        nc.sync.dma_start(out=scale[:], in_=hdn_scale.rearrange("a o k -> (a o k)").partition_broadcast(P))
+        nc.sync.dma_start(out=bias_rows[0:8, :], in_=fc2_b.rearrange("(j c) -> j c", j=8))
         nc.sync.dma_start(
             out=fc2_words[:].rearrange("p (g b) -> p g b", g=2), in_=fc2_w_words.rearrange("g p b -> p g b")
         )
@@ -84,12 +83,14 @@ def tile_tokenmudule_pb_w4_kernel(
                 out=fc2_scales[32 * q : 32 * q + 4, :].bitcast(I32).rearrange("q (g n) -> q g n", g=2),
                 in_=fc2_w_scales[:, 4 * q : 4 * q + 4, :].bitcast(I32).rearrange("g q n -> q g n"),
             )
-        nc.sync.dma_start(out=bias_rows[0:8, :], in_=fc2_b.rearrange("(j c) -> j c", j=8))
-        for s in range(2, 4):
+        for s in range(1, 4):
             load(s, 1)
 
         rbank = [psum.tile([P, 512], F32, name="rbank%d" % h, tag="r%d" % h) for h in range(2)]
         xw, xt, grp, codes, csc, tok, y, sq, cube = {}, {}, {}, {}, {}, {}, {}, {}, {}
+
+        def place(i):
+            return (i // 2, i % 2, 2) if i < 4 else (i // 4 + 1, i % 4, 4)
 
         def widen(i):
             xw[i] = work.tile([P, HIDDEN], BF16, name="xw", bufs=6, align_bytes=64)
@@ -112,50 +113,62 @@ def tile_tokenmudule_pb_w4_kernel(
                     nc.tensor.transpose(xt[i][:, 2 * g + u, :], words[:, 256 * g + u : 256 * (g + 1) : 2], ident[:])
 
         def empty(i):
-            s = i // 4
-            if i % 4 == 0:
+            s, q, size = place(i)
+            if q == 0:
                 grp[s] = work.tile([P, 4 * HIDDEN], BF16, name="grp", bufs=2, align_bytes=64)
+            used = grp[s][:, 0 : size * HIDDEN]
             if i < EARLY:
-                rows = grp[s][:].rearrange("p (g i b u e) -> p g i b u e", g=2, i=4, b=P, u=2)
+                rows = used.rearrange("p (g i b u e) -> p g i b u e", g=2, i=size, b=P, u=2)
                 for g in range(2):
                     nc.vector.tensor_tensor(
-                        out=rows[:, g, i % 4, :, :, :],
+                        out=rows[:, g, q, :, :, :],
                         in0=xt[i][:, 2 * g : 2 * g + 2, :].bitcast(BF16).rearrange("p u (b e) -> p b u e", e=2),
                         in1=scale_turned[:, 4 * g : 4 * g + 4]
                         .rearrange("p (o u e) -> p o u e", o=1, u=2)
                         .to_broadcast([P, P, 2, 2]),
                         op=ALU.mult,
                     )
-                return
-            view = grp[s][:].bitcast(F32).rearrange("p (g i b u) -> p g i b u", g=2, i=4, b=P)
-            nc.scalar.copy(out=view[:, :, i % 4, :, :], in_=xt[i][:].rearrange("p (g u) b -> p g b u", g=2))
+            else:
+                view = used.bitcast(F32).rearrange("p (g i b u) -> p g i b u", g=2, i=size, b=P)
+                nc.scalar.copy(out=view[:, :, q, :, :], in_=xt[i][:].rearrange("p (g u) b -> p g b u", g=2))
 
-        def quantize(s):
+        def quantize(s, size):
+            n = 256 * size
             codes[s] = work.tile([P, 1024], U32, name="codes", bufs=3, align_bytes=64)
             csc[s] = work.tile([P, 1024], U8, name="csc", bufs=3, align_bytes=64)
-            nc.vector.quantize_mx(out=codes[s][:].bitcast(FP8X4), scales=csc[s][:], in_=grp[s][:])
+            nc.vector.quantize_mx(
+                out=codes[s][:, 0:n].bitcast(FP8X4), scales=csc[s][:, 0:n], in_=grp[s][:, 0 : 4 * n]
+            )
+
+        def pieces(w):
+            if w < 4:
+                return [(jj // 2, 4 * (w % 2) + jj, 256 * jj, 256) for jj in range(4)]
+            return [(e, 2 * (w % 4) + e, 512 * e, 512) for e in range(2)]
 
         def multiply(w):
-            s = w // 4
+            s, q, size = place(w)
             for e in range(2):
                 tok[w, e] = psum.tile([P, 512], F32, name="tok", tag="t%d" % (2 * (w % 2) + e))
-                c0 = (2 * (w % 4) + e) * P
-                for g in range(2):
-                    col = g * CHANNELS + c0
-                    nc.tensor.matmul_mx(
-                        out=tok[w, e][:],
-                        lhsT=fc2_words[:, 2 * col : 2 * col + 256].bitcast(FP4X4),
-                        lhsT_scale=fc2_scales[:, col : col + P],
-                        rhs=codes[s][:, 512 * g : 512 * (g + 1)].bitcast(FP8X4),
-                        rhs_scale=csc[s][:, 512 * g : 512 * (g + 1)],
-                        start=(g == 0),
-                        stop=(g == 1),
-                    )
+            n = 128 if size == 2 else 512
+            for e, j, a, width in pieces(w):
+                for a1 in range(0, width, n):
+                    for g in range(2):
+                        col = g * CHANNELS + j * P
+                        x0 = g * 128 * size + a1
+                        nc.tensor.matmul_mx(
+                            out=tok[w, e][:, a + a1 - 512 * e : a + a1 - 512 * e + n],
+                            lhsT=fc2_words[:, 2 * col : 2 * col + 256].bitcast(FP4X4),
+                            lhsT_scale=fc2_scales[:, col : col + P],
+                            rhs=codes[s][:, x0 : x0 + n].bitcast(FP8X4),
+                            rhs_scale=csc[s][:, x0 : x0 + n],
+                            start=(g == 0),
+                            stop=(g == 1),
+                        )
 
         def late(w):
-            if w >= 34:
+            if w >= 33:
                 return (0, 1)
-            return (1,) if w >= 28 or w % 2 == 1 else ()
+            return (1,) if w >= 32 or (w >= 2 and w % 2 == 1) else ()
 
         def half(e):
             return slice(512 * e, 512 * e + 512)
@@ -163,15 +176,15 @@ def tile_tokenmudule_pb_w4_kernel(
         def first_scalar(w):
             y[w] = work.tile([P, 1024], F32, name="y", bufs=5)
             sq[w] = work.tile([P, 1024], F32, name="sq", bufs=5)
-            for e in range(2):
-                c = 2 * (w % 4) + e
+            for e, j, a, n in pieces(w):
+                source = tok[w, e][:, a - 512 * e : a - 512 * e + n]
                 if e in late(w):
                     nc.scalar.activation(
-                        out=sq[w][:, half(e)], in_=tok[w, e][:], func=ACT.Square, bias=bias[:, c : c + 1]
+                        out=sq[w][:, a : a + n], in_=source, func=ACT.Square, bias=bias[:, j : j + 1]
                     )
                 else:
                     nc.scalar.activation(
-                        out=y[w][:, half(e)], in_=tok[w, e][:], func=ACT.Relu, bias=bias_less[:, c : c + 1]
+                        out=y[w][:, a : a + n], in_=source, func=ACT.Relu, bias=bias_less[:, j : j + 1]
                     )
 
         def second_scalar(w):
@@ -181,12 +194,12 @@ def tile_tokenmudule_pb_w4_kernel(
 
         def late_product(w):
             cube[w] = work.tile([P, 1024], F32, name="cube", bufs=6)
-            for e in late(w):
-                c = 2 * (w % 4) + e
-                nc.vector.scalar_tensor_tensor(
-                    out=cube[w][:, half(e)], in0=tok[w, e][:], scalar=bias[:, c : c + 1],
-                    in1=sq[w][:, half(e)], op0=ALU.add, op1=ALU.mult,
-                )
+            for e, j, a, n in pieces(w):
+                if e in late(w):
+                    nc.vector.scalar_tensor_tensor(
+                        out=cube[w][:, a : a + n], in0=tok[w, e][:, a - 512 * e : a - 512 * e + n],
+                        scalar=bias[:, j : j + 1], in1=sq[w][:, a : a + n], op0=ALU.add, op1=ALU.mult,
+                    )
 
         def late_clip(w):
             for e in late(w):
@@ -201,33 +214,30 @@ def tile_tokenmudule_pb_w4_kernel(
                     out=cube[w][:, 0:n], in0=y[w][:, 0:n], scalar=EPS, in1=sq[w][:, 0:n], op0=ALU.add, op1=ALU.mult
                 )
 
+        def pool(w):
+            for e, j, a, n in pieces(w):
+                h, jj = divmod(j, 4)
+                for i in range(n // P):
+                    nc.tensor.matmul(
+                        out=rbank[h][:, P * jj : P * jj + P], lhsT=cube[w][:, a + P * i : a + P * i + P],
+                        rhs=ident[:], is_transpose=True, start=(w < 2 and jj == 0 and i == 0),
+                        stop=(w >= 32 and jj == 3 and i == 3),
+                    )
+
         def keep_warm(tag, count):
             warm = psum.tile([P, 512], F32, name="warm", tag=tag)
             for n in range(count):
                 nc.tensor.matmul(warm[:], lhsT=quiet[:, 0:P], rhs=quiet[:], start=True, stop=True)
 
-        def pool(w):
-            for e in range(2):
-                j = 2 * (w % 4) + e
-                h, jj = divmod(j, 4)
-                for i in range(4):
-                    a = 512 * e + P * i
-                    nc.tensor.matmul(
-                        out=rbank[h][:, P * jj : P * jj + P], lhsT=cube[w][:, a : a + P], rhs=ident[:],
-                        is_transpose=True, start=(w < 4 and jj == 0 and i == 0),
-                        stop=(w >= 32 and jj == 3 and i == 3),
-                    )
-
         def prepare_bias():
             nc.vector.tensor_copy(out=bias_rows32[:], in_=bias_rows[:])
-            turned = psum.tile([P, P], F32, name="turned", tag="t0")
+            turned = psum.tile([P, P], F32, name="turned", tag="t3")
             nc.tensor.transpose(turned[:], bias_rows32[:], ident[:])
             nc.vector.tensor_copy(out=bias[:], in_=turned[:, 0:8])
             nc.vector.tensor_scalar(out=bias_less[:], in0=bias[:], scalar1=-EPS, scalar2=None, op0=ALU.add)
 
-        pairs = 4 * STEPS
-        for k in range(pairs + 13):
-            w = k - 8
+        unit_at = {w + (4 if w < 2 else 5): w for w in range(4 * STEPS)}
+        for k in range(4 * STEPS + 9):
             if k % 2 == 0 and 4 <= k // 2 + 3 < STEPS:
                 load(k // 2 + 3, 1)
             if k == 12:
@@ -241,32 +251,35 @@ def tile_tokenmudule_pb_w4_kernel(
                         in_=head_w_scales[:, 4 * q : 4 * q + 4, :].bitcast(I32).rearrange("g q n -> q g n"),
                     )
                 nc.sync.dma_start(out=head_bias[:], in_=head_b.partition_broadcast(P))
-            if k == 6:
-                prepare_bias()
-            if k in (5, 6, 7):
-                keep_warm("t3", 3)
-            if 0 <= w < pairs:
-                multiply(w)
-            if k % 4 == 2 and 0 <= (k - 6) // 4 < STEPS:
-                quantize((k - 6) // 4)
+            w0, w1, w2, w3 = (unit_at.get(k - lag) for lag in range(4))
             if k < TOKENS:
                 widen(k)
-            if 0 <= w - 4 < pairs:
-                pool(w - 4)
-            if 0 <= k - 2 < TOKENS:
-                turn(k - 2)
-            if 0 <= w < pairs:
-                first_scalar(w)
-            if 0 <= k - 2 < TOKENS:
-                empty(k - 2)
-            if 0 <= w - 1 < pairs:
-                second_scalar(w - 1)
-            if 0 <= w - 2 < pairs:
-                product(w - 2)
-            if 0 <= w - 1 < pairs:
-                late_clip(w - 1)
-            if 0 <= w < pairs:
-                late_product(w)
+            if k == 1:
+                nc.scalar.dma_start(out=scale[:], in_=hdn_scale.rearrange("a o k -> (a o k)").partition_broadcast(P))
+            if k == 3:
+                prepare_bias()
+            if w0 is not None:
+                multiply(w0)
+            if 0 < k <= TOKENS:
+                s, q, size = place(k - 1)
+                if q == size - 1:
+                    quantize(s, size)
+            if w3 is not None:
+                pool(w3)
+            if w2 is not None:
+                late_clip(w2)
+            if k < TOKENS:
+                turn(k)
+            if w0 is not None:
+                first_scalar(w0)
+            if k < TOKENS:
+                empty(k)
+            if w0 is not None:
+                second_scalar(w0)
+            if w1 is not None:
+                late_product(w1)
+            if w2 is not None:
+                product(w2)
 
         logs = keep.tile([P, CHANNELS], F32, name="logs")
         g_bf = keep.tile([P, CHANNELS], BF16, name="g_bf", align_bytes=64)

from contextlib import ExitStack

import concourse.mybir as mybir
from concourse.masks import make_identity

IMAGES, TOKENS, HIDDEN, CHANNELS, OUT = 128, 36, 1024, 1024, 4096
FLOPS = 2 * IMAGES * TOKENS * HIDDEN * CHANNELS + 2 * IMAGES * CHANNELS * OUT

F32 = mybir.dt.float32
BF16 = mybir.dt.bfloat16
I32 = mybir.dt.int32
U32 = mybir.dt.uint32
U8 = mybir.dt.uint8
FP8 = mybir.dt.float8_e4m3fn
FP8X4 = mybir.dt.float8_e4m3fn_x4
FP4X4 = mybir.dt.float4_e2m1fn_x4
ALU = mybir.AluOpType
ACT = mybir.ActivationFunctionType

P = 128
EPS = 1e-6
EPS_CUBE = 1e-18
STEPS = 9
EARLY = 4


def tile_tokenmudule_pb_w4_kernel(
    tc, hdn_bytes, hdn_scale, fc2_w_words, fc2_w_scales, fc2_b, head_w_words, head_w_scales, head_b, out
):
    nc = tc.nc
    with ExitStack() as ctx:
        keep = ctx.enter_context(tc.tile_pool(name="keep", bufs=1))
        work = ctx.enter_context(tc.tile_pool(name="work", bufs=2))
        psum = ctx.enter_context(tc.psum_pool(name="psum", bufs=1))
        ctx.enter_context(tc.manual_schedule())

        ident = keep.tile([P, P], F32, name="ident")
        scale = keep.tile([P, HIDDEN], F32, name="scale")
        scale_turned = keep.tile([P, 8], F32, name="scale_turned")
        fc2_words = keep.tile([P, 2 * 2 * CHANNELS], U8, name="fc2_words", align_bytes=64)
        fc2_scales = keep.tile([P, 2 * CHANNELS], U8, name="fc2_scales", align_bytes=64)
        head_words = keep.tile([P, 2 * 2 * OUT], U8, name="head_words", align_bytes=64)
        head_scales = keep.tile([P, 2 * OUT], U8, name="head_scales", align_bytes=64)
        head_bias = keep.tile([P, OUT], BF16, name="head_bias")
        bias_rows = keep.tile([P, P], BF16, name="bias_rows")
        bias_rows32 = keep.tile([P, P], F32, name="bias_rows32")
        bias = keep.tile([P, 8], F32, name="bias")
        bias_less = keep.tile([P, 8], F32, name="bias_less")
        quiet = keep.tile([P, 512], BF16, name="quiet")
        one = keep.tile([P, 1], F32, name="one")
        junk = keep.tile([P, 1], F32, name="junk")

        nc.vector.memset(one[:], 1.0)
        nc.scalar.dma_start(
            out=scale_turned[:].rearrange("p (g t) -> p g t", g=2),
            in_=hdn_scale.rearrange("a o (g p t) -> p (a o g) t", g=2, p=P),
        )
        nc.scalar.activation(out=junk[:], in_=one[:], func=ACT.Ln)
        make_identity(nc, ident[:])
        nc.vector.memset(fc2_scales[:].bitcast(I32), 0)
        nc.vector.memset(bias_rows[:], 0.0)
        nc.gpsimd.memset(quiet[:], 0.0)
        nc.gpsimd.memset(head_scales[:].bitcast(I32), 0)

        xb = {}

        def load(s, pieces):
            xb[s] = work.tile([P, 4 * HIDDEN], U8, name="xb", bufs=6)
            n = 4 // pieces
            for q in range(pieces):
                nc.sync.dma_start(
                    out=xb[s][:, q * n * HIDDEN : (q + 1) * n * HIDDEN],
                    in_=hdn_bytes[:, 4 * s + q * n : 4 * s + (q + 1) * n, :].rearrange("b i k -> b (i k)"),
                )

        load(0, 4)
        nc.sync.dma_start(out=bias_rows[0:8, :], in_=fc2_b.rearrange("(j c) -> j c", j=8))
        nc.sync.dma_start(
            out=fc2_words[:].rearrange("p (g b) -> p g b", g=2), in_=fc2_w_words.rearrange("g p b -> p g b")
        )
        for q in range(4):
            nc.sync.dma_start(
                out=fc2_scales[32 * q : 32 * q + 4, :].bitcast(I32).rearrange("q (g n) -> q g n", g=2),
                in_=fc2_w_scales[:, 4 * q : 4 * q + 4, :].bitcast(I32).rearrange("g q n -> q g n"),
            )
        for s in range(1, 4):
            load(s, 1)

        rbank = [psum.tile([P, 512], F32, name="rbank%d" % h, tag="r%d" % h) for h in range(2)]
        xw, xt, grp, codes, csc, tok, y, sq, cube = {}, {}, {}, {}, {}, {}, {}, {}, {}

        def place(i):
            return (i // 2, i % 2, 2) if i < 4 else (i // 4 + 1, i % 4, 4)

        def widen(i):
            xw[i] = work.tile([P, HIDDEN], BF16, name="xw", bufs=6, align_bytes=64)
            q = i % 4
            values = xb[i // 4][:, q * HIDDEN : (q + 1) * HIDDEN].bitcast(FP8)
            if i == 0:
                for g in range(2):
                    half = slice(512 * g, 512 * g + 512)
                    nc.scalar.copy(out=xw[i][:, half], in_=values[:, half])
            elif i < EARLY:
                nc.scalar.copy(out=xw[i][:], in_=values)
            else:
                nc.vector.tensor_tensor(out=xw[i][:], in0=values, in1=scale[:], op=ALU.mult)

        def turn(i):
            xt[i] = psum.tile([P, 4, P], F32, name="xt", tag="x%d" % (i % 2))
            words = xw[i][:].bitcast(F32)
            for g in range(2):
                for u in range(2):
                    nc.tensor.transpose(xt[i][:, 2 * g + u, :], words[:, 256 * g + u : 256 * (g + 1) : 2], ident[:])

        def empty(i):
            s, q, size = place(i)
            if q == 0:
                grp[s] = work.tile([P, 4 * HIDDEN], BF16, name="grp", bufs=2, align_bytes=64)
            used = grp[s][:, 0 : size * HIDDEN]
            if i < EARLY:
                rows = used.rearrange("p (g i b u e) -> p g i b u e", g=2, i=size, b=P, u=2)
                for g in range(2):
                    nc.vector.tensor_tensor(
                        out=rows[:, g, q, :, :, :],
                        in0=xt[i][:, 2 * g : 2 * g + 2, :].bitcast(BF16).rearrange("p u (b e) -> p b u e", e=2),
                        in1=scale_turned[:, 4 * g : 4 * g + 4]
                        .rearrange("p (o u e) -> p o u e", o=1, u=2)
                        .to_broadcast([P, P, 2, 2]),
                        op=ALU.mult,
                    )
            else:
                view = used.bitcast(F32).rearrange("p (g i b u) -> p g i b u", g=2, i=size, b=P)
                nc.scalar.copy(out=view[:, :, q, :, :], in_=xt[i][:].rearrange("p (g u) b -> p g b u", g=2))

        def quantize(s, size):
            n = 256 * size
            codes[s] = work.tile([P, 1024], U32, name="codes", bufs=3, align_bytes=64)
            csc[s] = work.tile([P, 1024], U8, name="csc", bufs=3, align_bytes=64)
            nc.vector.quantize_mx(
                out=codes[s][:, 0:n].bitcast(FP8X4), scales=csc[s][:, 0:n], in_=grp[s][:, 0 : 4 * n]
            )

        def pieces(w):
            if w < 4:
                return [(jj // 2, 4 * (w % 2) + jj, 256 * jj, 256) for jj in range(4)]
            return [(e, 2 * (w % 4) + e, 512 * e, 512) for e in range(2)]

        def multiply(w):
            s, q, size = place(w)
            for e in range(2):
                tok[w, e] = psum.tile([P, 512], F32, name="tok", tag="t%d" % (2 * (w % 2) + e))
            n = 128 if size == 2 else 512
            for e, j, a, width in pieces(w):
                for a1 in range(0, width, n):
                    for g in range(2):
                        col = g * CHANNELS + j * P
                        x0 = g * 128 * size + a1
                        nc.tensor.matmul_mx(
                            out=tok[w, e][:, a + a1 - 512 * e : a + a1 - 512 * e + n],
                            lhsT=fc2_words[:, 2 * col : 2 * col + 256].bitcast(FP4X4),
                            lhsT_scale=fc2_scales[:, col : col + P],
                            rhs=codes[s][:, x0 : x0 + n].bitcast(FP8X4),
                            rhs_scale=csc[s][:, x0 : x0 + n],
                            start=(g == 0),
                            stop=(g == 1),
                        )

        def late(w):
            if w >= 33:
                return (0, 1)
            return (1,) if w >= 32 or (w >= 2 and w % 2 == 1) else ()

        def half(e):
            return slice(512 * e, 512 * e + 512)

        def first_scalar(w):
            y[w] = work.tile([P, 1024], F32, name="y", bufs=5)
            sq[w] = work.tile([P, 1024], F32, name="sq", bufs=5)
            for e, j, a, n in pieces(w):
                source = tok[w, e][:, a - 512 * e : a - 512 * e + n]
                if e in late(w):
                    nc.scalar.activation(
                        out=sq[w][:, a : a + n], in_=source, func=ACT.Square, bias=bias[:, j : j + 1]
                    )
                else:
                    nc.scalar.activation(
                        out=y[w][:, a : a + n], in_=source, func=ACT.Relu, bias=bias_less[:, j : j + 1]
                    )

        def second_scalar(w):
            n = 1024 - 512 * len(late(w))
            if n:
                nc.scalar.activation(out=sq[w][:, 0:n], in_=y[w][:, 0:n], func=ACT.Square, bias=EPS)

        def late_product(w):
            cube[w] = work.tile([P, 1024], F32, name="cube", bufs=6)
            for e, j, a, n in pieces(w):
                if e in late(w):
                    nc.vector.scalar_tensor_tensor(
                        out=cube[w][:, a : a + n], in0=tok[w, e][:, a - 512 * e : a - 512 * e + n],
                        scalar=bias[:, j : j + 1], in1=sq[w][:, a : a + n], op0=ALU.add, op1=ALU.mult,
                    )

        def late_clip(w):
            for e in late(w):
                nc.vector.tensor_scalar(
                    out=cube[w][:, half(e)], in0=cube[w][:, half(e)], scalar1=EPS_CUBE, scalar2=None, op0=ALU.max
                )

        def product(w):
            n = 1024 - 512 * len(late(w))
            if n:
                nc.vector.scalar_tensor_tensor(
                    out=cube[w][:, 0:n], in0=y[w][:, 0:n], scalar=EPS, in1=sq[w][:, 0:n], op0=ALU.add, op1=ALU.mult
                )

        def pool(w):
            for e, j, a, n in pieces(w):
                h, jj = divmod(j, 4)
                for i in range(n // P):
                    nc.tensor.matmul(
                        out=rbank[h][:, P * jj : P * jj + P], lhsT=cube[w][:, a + P * i : a + P * i + P],
                        rhs=ident[:], is_transpose=True, start=(w < 2 and jj == 0 and i == 0),
                        stop=(w >= 32 and jj == 3 and i == 3),
                    )

        def keep_warm(tag, count):
            warm = psum.tile([P, 512], F32, name="warm", tag=tag)
            for n in range(count):
                nc.tensor.matmul(warm[:], lhsT=quiet[:, 0:P], rhs=quiet[:], start=True, stop=True)

        def prepare_bias():
            nc.vector.tensor_copy(out=bias_rows32[:], in_=bias_rows[:])
            turned = psum.tile([P, P], F32, name="turned", tag="t3")
            nc.tensor.transpose(turned[:], bias_rows32[:], ident[:])
            nc.vector.tensor_copy(out=bias[:], in_=turned[:, 0:8])
            nc.vector.tensor_scalar(out=bias_less[:], in0=bias[:], scalar1=-EPS, scalar2=None, op0=ALU.add)

        unit_at = {w + (4 if w < 2 else 5): w for w in range(4 * STEPS)}
        for k in range(4 * STEPS + 9):
            if k % 2 == 0 and 4 <= k // 2 + 3 < STEPS:
                load(k // 2 + 3, 1)
            if k == 12:
                nc.sync.dma_start(
                    out=head_words[:].bitcast(I32).rearrange("p (g b) -> p g b", g=2),
                    in_=head_w_words.bitcast(I32).rearrange("g p b -> p g b"),
                )
                for q in range(4):
                    nc.sync.dma_start(
                        out=head_scales[32 * q : 32 * q + 4, :].bitcast(I32).rearrange("q (g n) -> q g n", g=2),
                        in_=head_w_scales[:, 4 * q : 4 * q + 4, :].bitcast(I32).rearrange("g q n -> q g n"),
                    )
                nc.sync.dma_start(out=head_bias[:], in_=head_b.partition_broadcast(P))
            w0, w1, w2, w3 = (unit_at.get(k - lag) for lag in range(4))
            if k < TOKENS:
                widen(k)
            if k == 1:
                nc.scalar.dma_start(out=scale[:], in_=hdn_scale.rearrange("a o k -> (a o k)").partition_broadcast(P))
            if k == 3:
                prepare_bias()
            if w0 is not None:
                multiply(w0)
            if 0 < k <= TOKENS:
                s, q, size = place(k - 1)
                if q == size - 1:
                    quantize(s, size)
            if w3 is not None:
                pool(w3)
            if w2 is not None:
                late_clip(w2)
            if k < TOKENS:
                turn(k)
            if w0 is not None:
                first_scalar(w0)
            if k < TOKENS:
                empty(k)
            if w0 is not None:
                second_scalar(w0)
            if w1 is not None:
                late_product(w1)
            if w2 is not None:
                product(w2)

        logs = keep.tile([P, CHANNELS], F32, name="logs")
        g_bf = keep.tile([P, CHANNELS], BF16, name="g_bf", align_bytes=64)
        g_grp = keep.tile([P, CHANNELS], BF16, name="g_grp", align_bytes=64)
        g_codes = keep.tile([P, 2 * P], U32, name="g_codes", align_bytes=64)
        g_scales = keep.tile([P, 2 * P], U8, name="g_scales", align_bytes=64)
        d = keep.tile([P, OUT], F32, name="d")
        res = keep.tile([P, OUT], F32, name="res")
        waste = keep.tile([P, 512], F32, name="waste")
        parts = keep.tile([P, 8], F32, name="parts")
        last_part = keep.tile([P, 1], F32, name="last_part")
        seven = keep.tile([P, 1], F32, name="seven")
        nc.gpsimd.memset(parts[:, 7:8], 2.0**-110)
        floored = keep.tile([P, 1], F32, name="floored")
        norm = keep.tile([P, 1], F32, name="norm")
        inv = keep.tile([P, 1], F32, name="inv")

        for h in range(2):
            nc.scalar.activation(
                out=logs[:, 512 * h : 512 * h + 512], in_=rbank[h][:], func=ACT.Ln, scale=1.0 / TOKENS
            )
        for h in range(2):
            nc.scalar.activation(
                out=g_bf[:, 512 * h : 512 * h + 512], in_=logs[:, 512 * h : 512 * h + 512], func=ACT.Exp,
                scale=1.0 / 3.0,
            )
        nc.scalar.activation(out=junk[:], in_=one[:], func=ACT.Sqrt)
        keep_warm("t0", 12)
        for h in range(2):
            gt = psum.tile([P, 2, P], F32, name="gt", tag="x%d" % h)
            words = g_bf[:].bitcast(F32)
            for u in range(2):
                nc.tensor.transpose(gt[:, u, :], words[:, 256 * h + u : 256 * (h + 1) : 2], ident[:])
            if h == 1:
                keep_warm("t1", 2)
            cols = slice(512 * h, 512 * h + 512)
            nc.vector.tensor_copy(
                out=g_grp[:, cols].bitcast(F32).rearrange("p (b u) -> p b u", u=2),
                in_=gt[:].rearrange("p u b -> p b u"),
            )
            nc.vector.quantize_mx(
                out=g_codes[:, P * h : P * h + P].bitcast(FP8X4), scales=g_scales[:, P * h : P * h + P],
                in_=g_grp[:, cols],
            )
        tags = ["t0", "t1", "t2", "t3", "r0", "r1", "x0", "x1"]
        acc = [psum.tile([P, 512], F32, name="acc%d" % n, tag=tags[n]) for n in range(8)]

        def head(n, g):
            col = g * OUT + 512 * n
            nc.tensor.matmul_mx(
                out=acc[n][:],
                lhsT=g_codes[:, P * g : P * g + P].bitcast(FP8X4),
                lhsT_scale=g_scales[:, P * g : P * g + P],
                rhs=head_words[:, 2 * col : 2 * col + 1024].bitcast(FP4X4),
                rhs_scale=head_scales[:, col : col + 512],
                start=(g == 0),
                stop=(g == 1),
            )

        for n0 in range(0, 8, 2):
            for g in range(2):
                for n in (n0, n0 + 1):
                    head(n, g)
        for n in range(8):
            cols = slice(512 * n, 512 * n + 512)
            nc.vector.tensor_tensor(out=d[:, cols], in0=acc[n][:], in1=head_bias[:, cols], op=ALU.add)
            nc.scalar.activation(out=waste[:], in_=d[:, cols], func=ACT.Square, accum_out=last_part[:] if n == 7 else parts[:, n : n + 1])
            if n == 7:
                nc.vector.tensor_reduce(out=seven[:], in_=parts[:], axis=mybir.AxisListType.X, op=ALU.add)
        nc.scalar.activation(out=norm[:], in_=last_part[:], func=ACT.Sqrt, bias=seven[:])
        nc.vector.tensor_scalar(out=floored[:], in0=norm[:], scalar1=1e-12, scalar2=None, op0=ALU.max)
        nc.vector.reciprocal(out=inv[:], in_=floored[:])
        for n in range(8):
            cols = slice(512 * n, 512 * n + 512)
            if n in (2, 5, 7):
                nc.scalar.activation(out=res[:, cols], in_=d[:, cols], func=ACT.Copy, scale=inv[:, 0:1])
            else:
                nc.vector.tensor_scalar(
                    out=res[:, cols], in0=d[:, cols], scalar1=inv[:, 0:1], scalar2=None, op0=ALU.mult
                )
        for n in (0, 2, 1, 3, 5, 4, 6, 7):
            cols = slice(512 * n, 512 * n + 512)
            nc.sync.dma_start(out=out[:, cols], in_=res[:, cols])
